import numpy as np
import ml_dtypes

BF16 = ml_dtypes.bfloat16


def bf(x):
    return np.asarray(x, np.float32).astype(BF16)


def f32(x):
    return np.asarray(x, np.float32)


def f64(x):
    return np.asarray(x).astype(np.float64)


def striped(idx):
    return np.tile(idx.reshape(-1, 16).T, (8, 1))


C0, C1, D, C3, M, S, H, K, N = 512, 256, 128, 256, 256, 1024, 512, 8, 4096
EPS = 1e-5


def draw(c, n):
    return 0.5 * np.random.standard_normal((c, 1)) + (0.75 + 0.5 * np.random.random((c, 1))) * np.random.standard_normal((c, n))


def params(c):
    gamma = f32(0.25 * (1.0 + 0.1 * np.random.standard_normal((c, 1))))
    beta = f32(0.1 * np.random.standard_normal((c, 1)))
    w = bf(np.random.standard_normal((c, M)) / np.sqrt(c))
    return gamma, beta, w


def bn(f, gamma, beta):
    mean = f.mean(axis=1, keepdims=True)
    var = np.square(f - mean).mean(axis=1, keepdims=True)
    return (f - mean) / np.sqrt(var + EPS) * gamma + beta


def setup_inputs():
    d = {}
    d["f0"] = f32(draw(C0, N))
    d["gamma0"], d["beta0"], d["w0"] = params(C0)
    d["f1"] = f32(draw(C1, N))
    d["gamma1"], d["beta1"], d["w1"] = params(C1)
    d["table"] = bf(draw(D, S).T)
    d["gamma2"], d["beta2"], d["w2"] = params(D)
    d["f3"] = f32(draw(C3, N))
    d["gamma3"], d["beta3"], d["w3"] = params(C3)
    d["offs"] = striped(np.concatenate([np.random.permutation(S)[:H] for _ in range(K)]))
    return d


def reference(f0, gamma0, beta0, w0, f1, gamma1, beta1, w1, table, gamma2, beta2, w2, f3, gamma3, beta3, w3, offs):
    idx = offs[:16].T.reshape(-1)
    acc = f64(w0).T @ bn(f64(f0), f64(gamma0), f64(beta0))
    acc = f64(w1).T @ bn(f64(f1), f64(gamma1), f64(beta1)) + acc
    acc = f64(w2).T @ bn(f64(table).T, f64(gamma2), f64(beta2))[:, idx] + acc
    acc = f64(w3).T @ bn(f64(f3), f64(gamma3), f64(beta3)) + acc
    return acc

@@ -1,0 +1,169 @@
+import concourse.mybir as mybir
+from concourse.masks import make_identity
+
+F32, BF16, U16 = mybir.dt.float32, mybir.dt.bfloat16, mybir.dt.uint16
+MULT, ADD = mybir.AluOpType.mult, mybir.AluOpType.add
+IDENTITY, SQRT = mybir.ActivationFunctionType.Identity, mybir.ActivationFunctionType.Sqrt
+
+P = 128
+POINTS = 4096
+COARSE = 1024
+FEATURES = 256
+PIECE = 512
+PIECES = POINTS // PIECE
+DENSE = 8
+TABLE = DENSE
+STAT = 512
+EPS = 1e-5
+LEAD = 3
+SCALAR_COLUMNS = 2560
+
+FLOPS = 2 * (DENSE + 1) * P * FEATURES * POINTS
+
+
+def tile_decoder_b_kernel(
+    tc, f0, gamma0, beta0, w0, f1, gamma1, beta1, w1, table, gamma2, beta2, w2,
+    f3, gamma3, beta3, w3, offs, out,
+):
+    nc = tc.nc
+    parameters = (
+        (gamma0, beta0, w0, 0),
+        (gamma1, beta1, w1, 4),
+        (gamma3, beta3, w3, 6),
+        (gamma2, beta2, w2, TABLE),
+    )
+
+    with (
+        tc.tile_pool(name="held", bufs=1) as held,
+        tc.tile_pool(name="raws", bufs=DENSE) as raws,
+        tc.tile_pool(name="normed", bufs=DENSE) as normed,
+        tc.tile_pool(name="small", bufs=DENSE + 1) as small,
+        tc.tile_pool(name="stage", bufs=4) as stage,
+    ):
+        offsets = held.tile([P, POINTS // 16], U16, name="offsets")
+        nc.sync.dma_start(offsets[:], offs)
+
+        table_rows = held.tile([P, COARSE // P, P], BF16, name="table_rows")
+        nc.sync.dma_start(table_rows[:], table.rearrange("(g p) d -> p g d", p=P))
+
+        weights = held.tile([P, DENSE + 1, FEATURES], BF16, name="weights")
+        param_rows = held.tile([P, P], F32, name="param_rows")
+        nc.vector.memset(param_rows[:], 0.0)
+        for gamma, beta, w, first in parameters:
+            blocks = w.shape[0] // P
+            nc.scalar.dma_start(
+                weights[:, first : first + blocks, :], w.rearrange("(k c) m -> c k m", c=P)
+            )
+            nc.scalar.dma_start(
+                param_rows[first : first + blocks, :], gamma.rearrange("(k c) o -> k (c o)", c=P)
+            )
+            nc.scalar.dma_start(
+                param_rows[DENSE + 1 + first : DENSE + 1 + first + blocks, :],
+                beta.rearrange("(k c) o -> k (c o)", c=P),
+            )
+
+        raw = []
+        for f in (f0, f1, f3):
+            for k in range(f.shape[0] // P):
+                block = raws.tile([P, POINTS], F32, name="raw")
+                for h in range(2):
+                    columns = slice(h * POINTS // 2, (h + 1) * POINTS // 2)
+                    nc.sync.dma_start(block[:, columns], f[k * P : (k + 1) * P, columns])
+                raw.append(block)
+
+        identity_bf16 = held.tile([P, P], BF16, name="identity_bf16")
+        make_identity(nc, identity_bf16[:])
+        identity_f32 = held.tile([P, P], F32, name="identity_f32")
+        make_identity(nc, identity_f32[:])
+        eps = held.tile([P, 1], F32, name="eps")
+        nc.vector.memset(eps[:], EPS)
+
+        gain = held.tile([P, DENSE + 1, 2], F32, name="gain")
+        bias = held.tile([P, DENSE + 1], F32, name="bias")
+        window = held.tile([P, COARSE], BF16, name="window")
+
+        def scale_and_shift(stats, k):
+            mean_var = small.tile([P, 2], F32, name="mean_var")
+            nc.vector.bn_aggr(mean_var[:], stats[:])
+            std = small.tile([P, 1], F32, name="std")
+            nc.scalar.activation(std[:], mean_var[:, 1:2], SQRT, bias=eps[:])
+            rstd = small.tile([P, 1], F32, name="rstd")
+            nc.vector.reciprocal(rstd[:], std[:])
+            scale = small.tile([P, 2], F32, name="scale")
+            nc.vector.tensor_scalar_mul(scale[:], gain[:, k, :], rstd[:])
+            shift = small.tile([P, 1], F32, name="shift")
+            nc.vector.tensor_scalar(
+                shift[:], mean_var[:, 0:1], scale[:, 1:2], bias[:, k : k + 1], MULT, ADD
+            )
+            return scale, shift
+
+        with tc.psum_pool(name="flips", bufs=1) as flips:
+            param_columns = flips.tile([P, P], F32, name="param_columns")
+            nc.tensor.transpose(param_columns[:], param_rows[:], identity_f32[:])
+            nc.vector.tensor_copy(gain[:, :, 0], param_columns[:, 0 : DENSE + 1])
+            nc.vector.tensor_scalar_mul(gain[:, :, 1], param_columns[:, 0 : DENSE + 1], -1.0)
+            nc.vector.tensor_copy(bias[:], param_columns[:, DENSE + 1 : 2 * (DENSE + 1)])
+
+            flipped = flips.tile([P, COARSE], BF16, name="flipped")
+            for g in range(COARSE // P):
+                nc.tensor.transpose(
+                    flipped[:, g * P : (g + 1) * P], table_rows[:, g, :], identity_bf16[:]
+                )
+            table_stats = small.tile([P, 6 * (COARSE // STAT)], F32, name="table_stats")
+            for c in range(COARSE // STAT):
+                nc.vector.bn_stats(
+                    table_stats[:, 6 * c : 6 * c + 6], flipped[:, c * STAT : (c + 1) * STAT]
+                )
+            scale, shift = scale_and_shift(table_stats, TABLE)
+            nc.scalar.activation(
+                window[:], flipped[:], IDENTITY, bias=shift[:], scale=scale[:, 0:1]
+            )
+
+        y = []
+        for k in range(DENSE):
+            stats = small.tile([P, 6 * (POINTS // STAT)], F32, name="stats")
+            for c in range(POINTS // STAT):
+                nc.vector.bn_stats(
+                    stats[:, 6 * c : 6 * c + 6], raw[k][:, c * STAT : (c + 1) * STAT]
+                )
+            scale, shift = scale_and_shift(stats, k)
+            block = normed.tile([P, POINTS], BF16, name="y")
+            nc.scalar.activation(
+                block[:, :SCALAR_COLUMNS], raw[k][:, :SCALAR_COLUMNS], IDENTITY,
+                bias=shift[:], scale=scale[:, 0:1],
+            )
+            nc.gpsimd.tensor_scalar(
+                block[:, SCALAR_COLUMNS:], raw[k][:, SCALAR_COLUMNS:],
+                scale[:, 0:1], shift[:], MULT, ADD,
+            )
+            y.append(block)
+
+        with tc.psum_pool(name="sums", bufs=PIECES) as sums:
+            for half, lead in enumerate((0, LEAD)):
+                features = slice(half * P, (half + 1) * P)
+                banks = [sums.tile([P, PIECE], F32, name="bank") for j in range(PIECES)]
+                for k in range(lead):
+                    for j in range(PIECES):
+                        nc.tensor.matmul(
+                            banks[j][:], weights[:, k, features],
+                            y[k][:, j * PIECE : (j + 1) * PIECE], start=(k == 0), stop=False,
+                        )
+                for j in range(PIECES):
+                    listed = offsets[:, j * (PIECE // 16) : (j + 1) * (PIECE // 16)]
+                    nc.tensor.matmul(
+                        banks[j][:], weights[:, TABLE, features], window[:].indirect(listed),
+                        start=(lead == 0), stop=False,
+                    )
+                for j in range(PIECES):
+                    points = slice(j * PIECE, (j + 1) * PIECE)
+                    for k in range(lead, DENSE):
+                        nc.tensor.matmul(
+                            banks[j][:], weights[:, k, features], y[k][:, points],
+                            start=False, stop=(k == DENSE - 1),
+                        )
+                    staged = stage.tile([P, PIECE], F32, name="staged")
+                    if j % 2 == 0:
+                        nc.scalar.copy(staged[:], banks[j][:])
+                    else:
+                        nc.vector.tensor_copy(staged[:], banks[j][:])
+                    nc.sync.dma_start(out[features, points], staged[:])

@@ -66,8 +66,8 @@ def tile_decoder_b_kernel(
         for f in (f0, f1, f3):
             for k in range(f.shape[0] // P):
                 block = raws.tile([P, POINTS], F32, name="raw")
-                for h in range(2):
-                    columns = slice(h * POINTS // 2, (h + 1) * POINTS // 2)
+                for c in range(POINTS // STAT):
+                    columns = slice(c * STAT, (c + 1) * STAT)
                     nc.sync.dma_start(block[:, columns], f[k * P : (k + 1) * P, columns])
                 raw.append(block)
 

@@ -15,6 +15,7 @@ DENSE = 8
 TABLE = DENSE
 STAT = 512
 EPS = 1e-5
+SPLIT = 3
 LEAD = 3
 SCALAR_COLUMNS = 2560
 
@@ -81,6 +82,7 @@ def tile_decoder_b_kernel(
         gain = held.tile([P, DENSE + 1, 2], F32, name="gain")
         bias = held.tile([P, DENSE + 1], F32, name="bias")
         window = held.tile([P, COARSE], BF16, name="window")
+        parked = held.tile([P, POINTS], F32, name="parked")
 
         def scale_and_shift(stats, k):
             mean_var = small.tile([P, 2], F32, name="mean_var")
@@ -96,6 +98,24 @@ def tile_decoder_b_kernel(
                 shift[:], mean_var[:, 0:1], scale[:, 1:2], bias[:, k : k + 1], MULT, ADD
             )
             return scale, shift
+
+        def normalised(k):
+            stats = small.tile([P, 6 * (POINTS // STAT)], F32, name="stats")
+            for c in range(POINTS // STAT):
+                nc.vector.bn_stats(
+                    stats[:, 6 * c : 6 * c + 6], raw[k][:, c * STAT : (c + 1) * STAT]
+                )
+            scale, shift = scale_and_shift(stats, k)
+            block = normed.tile([P, POINTS], BF16, name="y")
+            nc.scalar.activation(
+                block[:, :SCALAR_COLUMNS], raw[k][:, :SCALAR_COLUMNS], IDENTITY,
+                bias=shift[:], scale=scale[:, 0:1],
+            )
+            nc.gpsimd.tensor_scalar(
+                block[:, SCALAR_COLUMNS:], raw[k][:, SCALAR_COLUMNS:],
+                scale[:, 0:1], shift[:], MULT, ADD,
+            )
+            return block
 
         with tc.psum_pool(name="flips", bufs=1) as flips:
             param_columns = flips.tile([P, P], F32, name="param_columns")
@@ -119,51 +139,63 @@ def tile_decoder_b_kernel(
                 window[:], flipped[:], IDENTITY, bias=shift[:], scale=scale[:, 0:1]
             )
 
-        y = []
-        for k in range(DENSE):
-            stats = small.tile([P, 6 * (POINTS // STAT)], F32, name="stats")
-            for c in range(POINTS // STAT):
-                nc.vector.bn_stats(
-                    stats[:, 6 * c : 6 * c + 6], raw[k][:, c * STAT : (c + 1) * STAT]
-                )
-            scale, shift = scale_and_shift(stats, k)
-            block = normed.tile([P, POINTS], BF16, name="y")
-            nc.scalar.activation(
-                block[:, :SCALAR_COLUMNS], raw[k][:, :SCALAR_COLUMNS], IDENTITY,
-                bias=shift[:], scale=scale[:, 0:1],
-            )
-            nc.gpsimd.tensor_scalar(
-                block[:, SCALAR_COLUMNS:], raw[k][:, SCALAR_COLUMNS:],
-                scale[:, 0:1], shift[:], MULT, ADD,
-            )
-            y.append(block)
-
         with tc.psum_pool(name="sums", bufs=PIECES) as sums:
-            for half, lead in enumerate((0, LEAD)):
-                features = slice(half * P, (half + 1) * P)
-                banks = [sums.tile([P, PIECE], F32, name="bank") for j in range(PIECES)]
-                for k in range(lead):
-                    for j in range(PIECES):
-                        nc.tensor.matmul(
-                            banks[j][:], weights[:, k, features],
-                            y[k][:, j * PIECE : (j + 1) * PIECE], start=(k == 0), stop=False,
-                        )
+
+            def open_banks():
+                return [sums.tile([P, PIECE], F32, name="bank") for j in range(PIECES)]
+
+            def dense(bank, half, k, j, start, stop):
+                nc.tensor.matmul(
+                    bank[:], weights[:, k, half * P : (half + 1) * P],
+                    y[k][:, j * PIECE : (j + 1) * PIECE], start=start, stop=stop,
+                )
+
+            def gathered(bank, half, j, start):
+                listed = offsets[:, j * (PIECE // 16) : (j + 1) * (PIECE // 16)]
+                nc.tensor.matmul(
+                    bank[:], weights[:, TABLE, half * P : (half + 1) * P],
+                    window[:].indirect(listed), start=start, stop=False,
+                )
+
+            def store(staged, half, j):
+                nc.sync.dma_start(
+                    out[half * P : (half + 1) * P, j * PIECE : (j + 1) * PIECE], staged[:]
+                )
+
+
+            y = [normalised(k) for k in range(SPLIT)]
+            banks = open_banks()
+            for j in range(PIECES):
+                gathered(banks[j], 0, j, start=True)
+            for j in range(PIECES):
+                for k in range(SPLIT):
+                    dense(banks[j], 0, k, j, start=False, stop=(k == SPLIT - 1))
+                nc.scalar.copy(parked[:, j * PIECE : (j + 1) * PIECE], banks[j][:])
+
+            for k in range(SPLIT, DENSE):
+                y.append(normalised(k))
+            banks = open_banks()
+            for k in range(LEAD):
                 for j in range(PIECES):
-                    listed = offsets[:, j * (PIECE // 16) : (j + 1) * (PIECE // 16)]
-                    nc.tensor.matmul(
-                        banks[j][:], weights[:, TABLE, features], window[:].indirect(listed),
-                        start=(lead == 0), stop=False,
-                    )
-                for j in range(PIECES):
-                    points = slice(j * PIECE, (j + 1) * PIECE)
-                    for k in range(lead, DENSE):
-                        nc.tensor.matmul(
-                            banks[j][:], weights[:, k, features], y[k][:, points],
-                            start=False, stop=(k == DENSE - 1),
-                        )
-                    staged = stage.tile([P, PIECE], F32, name="staged")
-                    if j % 2 == 0:
-                        nc.scalar.copy(staged[:], banks[j][:])
-                    else:
-                        nc.vector.tensor_copy(staged[:], banks[j][:])
-                    nc.sync.dma_start(out[features, points], staged[:])
+                    dense(banks[j], 1, k, j, start=(k == 0), stop=False)
+            for j in range(PIECES):
+                gathered(banks[j], 1, j, start=False)
+            for j in range(PIECES):
+                for k in range(LEAD, DENSE):
+                    dense(banks[j], 1, k, j, start=False, stop=(k == DENSE - 1))
+                staged = stage.tile([P, PIECE], F32, name="staged")
+                if j % 2 == 0:
+                    nc.scalar.copy(staged[:], banks[j][:])
+                else:
+                    nc.vector.tensor_copy(staged[:], banks[j][:])
+                store(staged, 1, j)
+
+            banks = open_banks()
+            for j in range(PIECES):
+                for k in range(SPLIT, DENSE):
+                    dense(banks[j], 0, k, j, start=(k == SPLIT), stop=(k == DENSE - 1))
+                staged = stage.tile([P, PIECE], F32, name="staged")
+                nc.vector.tensor_tensor(
+                    staged[:], banks[j][:], parked[:, j * PIECE : (j + 1) * PIECE], ADD
+                )
+                store(staged, 0, j)

@@ -2,8 +2,8 @@ import concourse.mybir as mybir
 from concourse.masks import make_identity
 
 F32, BF16, U16 = mybir.dt.float32, mybir.dt.bfloat16, mybir.dt.uint16
-MULT, ADD = mybir.AluOpType.mult, mybir.AluOpType.add
-IDENTITY, SQRT = mybir.ActivationFunctionType.Identity, mybir.ActivationFunctionType.Sqrt
+MULT, ADD, POW = mybir.AluOpType.mult, mybir.AluOpType.add, mybir.AluOpType.pow
+IDENTITY = mybir.ActivationFunctionType.Identity
 
 P = 128
 POINTS = 4096
@@ -15,9 +15,7 @@ DENSE = 8
 TABLE = DENSE
 STAT = 512
 EPS = 1e-5
-SPLIT = 3
-LEAD = 3
-SCALAR_COLUMNS = 2560
+SPLIT = 4
 
 FLOPS = 2 * (DENSE + 1) * P * FEATURES * POINTS
 
@@ -28,33 +26,25 @@ def tile_decoder_b_kernel(
 ):
     nc = tc.nc
     parameters = (
+        (gamma2, beta2, w2, TABLE),
         (gamma0, beta0, w0, 0),
         (gamma1, beta1, w1, 4),
         (gamma3, beta3, w3, 6),
-        (gamma2, beta2, w2, TABLE),
     )
 
     with (
         tc.tile_pool(name="held", bufs=1) as held,
         tc.tile_pool(name="raws", bufs=DENSE) as raws,
         tc.tile_pool(name="normed", bufs=DENSE) as normed,
-        tc.tile_pool(name="small", bufs=DENSE + 1) as small,
-        tc.tile_pool(name="stage", bufs=4) as stage,
+        tc.tile_pool(name="small", bufs=4) as small,
     ):
-        offsets = held.tile([P, POINTS // 16], U16, name="offsets")
-        nc.sync.dma_start(offsets[:], offs)
-
         table_rows = held.tile([P, COARSE // P, P], BF16, name="table_rows")
         nc.sync.dma_start(table_rows[:], table.rearrange("(g p) d -> p g d", p=P))
 
-        weights = held.tile([P, DENSE + 1, FEATURES], BF16, name="weights")
         param_rows = held.tile([P, P], F32, name="param_rows")
         nc.vector.memset(param_rows[:], 0.0)
         for gamma, beta, w, first in parameters:
             blocks = w.shape[0] // P
-            nc.scalar.dma_start(
-                weights[:, first : first + blocks, :], w.rearrange("(k c) m -> c k m", c=P)
-            )
             nc.scalar.dma_start(
                 param_rows[first : first + blocks, :], gamma.rearrange("(k c) o -> k (c o)", c=P)
             )
@@ -62,7 +52,14 @@ def tile_decoder_b_kernel(
                 param_rows[DENSE + 1 + first : DENSE + 1 + first + blocks, :],
                 beta.rearrange("(k c) o -> k (c o)", c=P),
             )
+        weights = held.tile([P, DENSE + 1, FEATURES], BF16, name="weights")
+        for gamma, beta, w, first in parameters:
+            nc.scalar.dma_start(
+                weights[:, first : first + w.shape[0] // P, :],
+                w.rearrange("(k c) m -> c k m", c=P),
+            )
 
+        offsets = held.tile([P, POINTS // 16], U16, name="offsets")
         raw = []
         for f in (f0, f1, f3):
             for k in range(f.shape[0] // P):
@@ -70,31 +67,33 @@ def tile_decoder_b_kernel(
                 for c in range(POINTS // STAT):
                     columns = slice(c * STAT, (c + 1) * STAT)
                     nc.sync.dma_start(block[:, columns], f[k * P : (k + 1) * P, columns])
+                if not raw:
+                    nc.sync.dma_start(offsets[:], offs)
                 raw.append(block)
 
         identity_bf16 = held.tile([P, P], BF16, name="identity_bf16")
         make_identity(nc, identity_bf16[:])
         identity_f32 = held.tile([P, P], F32, name="identity_f32")
         make_identity(nc, identity_f32[:])
-        eps = held.tile([P, 1], F32, name="eps")
-        nc.vector.memset(eps[:], EPS)
+        minus_half = held.tile([P, 1], F32, name="minus_half")
+        nc.vector.memset(minus_half[:], -0.5)
 
         gain = held.tile([P, DENSE + 1, 2], F32, name="gain")
         bias = held.tile([P, DENSE + 1], F32, name="bias")
         window = held.tile([P, COARSE], BF16, name="window")
-        parked = held.tile([P, POINTS], F32, name="parked")
+        total = [held.tile([P, POINTS], F32, name=f"total{half}") for half in range(2)]
 
         def scale_and_shift(stats, k):
             mean_var = small.tile([P, 2], F32, name="mean_var")
             nc.vector.bn_aggr(mean_var[:], stats[:])
-            std = small.tile([P, 1], F32, name="std")
-            nc.scalar.activation(std[:], mean_var[:, 1:2], SQRT, bias=eps[:])
+            spread = small.tile([P, 1], F32, name="spread")
+            nc.gpsimd.tensor_scalar_add(spread[:], mean_var[:, 1:2], EPS)
             rstd = small.tile([P, 1], F32, name="rstd")
-            nc.vector.reciprocal(rstd[:], std[:])
+            nc.gpsimd.tensor_tensor(rstd[:], spread[:], minus_half[:], POW)
             scale = small.tile([P, 2], F32, name="scale")
-            nc.vector.tensor_scalar_mul(scale[:], gain[:, k, :], rstd[:])
+            nc.gpsimd.tensor_scalar_mul(scale[:], gain[:, k, :], rstd[:])
             shift = small.tile([P, 1], F32, name="shift")
-            nc.vector.tensor_scalar(
+            nc.gpsimd.tensor_scalar(
                 shift[:], mean_var[:, 0:1], scale[:, 1:2], bias[:, k : k + 1], MULT, ADD
             )
             return scale, shift
@@ -107,14 +106,23 @@ def tile_decoder_b_kernel(
                 )
             scale, shift = scale_and_shift(stats, k)
             block = normed.tile([P, POINTS], BF16, name="y")
-            nc.scalar.activation(
-                block[:, :SCALAR_COLUMNS], raw[k][:, :SCALAR_COLUMNS], IDENTITY,
-                bias=shift[:], scale=scale[:, 0:1],
-            )
-            nc.gpsimd.tensor_scalar(
-                block[:, SCALAR_COLUMNS:], raw[k][:, SCALAR_COLUMNS:],
-                scale[:, 0:1], shift[:], MULT, ADD,
-            )
+            scalar_pieces, vector_pieces = (5, 0) if k < DENSE - 1 else (3, 5)
+            for j in range(scalar_pieces + vector_pieces):
+                points = slice(j * PIECE, (j + 1) * PIECE)
+                if j < scalar_pieces:
+                    nc.scalar.activation(
+                        block[:, points], raw[k][:, points], IDENTITY,
+                        bias=shift[:], scale=scale[:, 0:1],
+                    )
+                else:
+                    nc.vector.tensor_scalar(
+                        block[:, points], raw[k][:, points], scale[:, 0:1], shift[:], MULT, ADD
+                    )
+            if scalar_pieces + vector_pieces < PIECES:
+                rest = slice((scalar_pieces + vector_pieces) * PIECE, POINTS)
+                nc.gpsimd.tensor_scalar(
+                    block[:, rest], raw[k][:, rest], scale[:, 0:1], shift[:], MULT, ADD
+                )
             return block
 
         with tc.psum_pool(name="flips", bufs=1) as flips:
@@ -144,58 +152,53 @@ def tile_decoder_b_kernel(
             def open_banks():
                 return [sums.tile([P, PIECE], F32, name="bank") for j in range(PIECES)]
 
-            def dense(bank, half, k, j, start, stop):
-                nc.tensor.matmul(
-                    bank[:], weights[:, k, half * P : (half + 1) * P],
-                    y[k][:, j * PIECE : (j + 1) * PIECE], start=start, stop=stop,
-                )
-
-            def gathered(bank, half, j, start):
+            def gathered(bank, half, j, stop):
                 listed = offsets[:, j * (PIECE // 16) : (j + 1) * (PIECE // 16)]
                 nc.tensor.matmul(
                     bank[:], weights[:, TABLE, half * P : (half + 1) * P],
-                    window[:].indirect(listed), start=start, stop=False,
+                    window[:].indirect(listed), start=True, stop=stop,
                 )
 
-            def store(staged, half, j):
-                nc.sync.dma_start(
-                    out[half * P : (half + 1) * P, j * PIECE : (j + 1) * PIECE], staged[:]
-                )
+            def dense(bank, half, j, blocks, start):
+                for k in blocks:
+                    nc.tensor.matmul(
+                        bank[:], weights[:, k, half * P : (half + 1) * P],
+                        y[k][:, j * PIECE : (j + 1) * PIECE],
+                        start=(start and k == blocks[0]), stop=(k == blocks[-1]),
+                    )
 
+            def park(bank, half, j, on_vector):
+                points = slice(j * PIECE, (j + 1) * PIECE)
+                if on_vector:
+                    nc.vector.tensor_copy(total[half][:, points], bank[:])
+                else:
+                    nc.scalar.copy(total[half][:, points], bank[:])
 
-            y = [normalised(k) for k in range(SPLIT)]
+            def finish(bank, half, j):
+                points = slice(j * PIECE, (j + 1) * PIECE)
+                nc.vector.tensor_tensor(total[half][:, points], bank[:], total[half][:, points], ADD)
+                nc.sync.dma_start(out[half * P : (half + 1) * P, points], total[half][:, points])
+
+            table_banks = open_banks()
+            for j in range(PIECES):
+                gathered(table_banks[j], 1, j, stop=True)
+                park(table_banks[j], 1, j, on_vector=(j % 2 == 1))
             banks = open_banks()
             for j in range(PIECES):
-                gathered(banks[j], 0, j, start=True)
+                gathered(banks[j], 0, j, stop=False)
+            y = [normalised(k) for k in range(SPLIT)]
             for j in range(PIECES):
-                for k in range(SPLIT):
-                    dense(banks[j], 0, k, j, start=False, stop=(k == SPLIT - 1))
-                nc.scalar.copy(parked[:, j * PIECE : (j + 1) * PIECE], banks[j][:])
+                dense(banks[j], 0, j, range(SPLIT), start=False)
+                park(banks[j], 0, j, on_vector=False)
 
             for k in range(SPLIT, DENSE):
                 y.append(normalised(k))
             banks = open_banks()
-            for k in range(LEAD):
-                for j in range(PIECES):
-                    dense(banks[j], 1, k, j, start=(k == 0), stop=False)
             for j in range(PIECES):
-                gathered(banks[j], 1, j, start=False)
-            for j in range(PIECES):
-                for k in range(LEAD, DENSE):
-                    dense(banks[j], 1, k, j, start=False, stop=(k == DENSE - 1))
-                staged = stage.tile([P, PIECE], F32, name="staged")
-                if j % 2 == 0:
-                    nc.scalar.copy(staged[:], banks[j][:])
-                else:
-                    nc.vector.tensor_copy(staged[:], banks[j][:])
-                store(staged, 1, j)
+                dense(banks[j], 1, j, range(DENSE), start=True)
+                finish(banks[j], 1, j)
 
             banks = open_banks()
             for j in range(PIECES):
-                for k in range(SPLIT, DENSE):
-                    dense(banks[j], 0, k, j, start=(k == SPLIT), stop=(k == DENSE - 1))
-                staged = stage.tile([P, PIECE], F32, name="staged")
-                nc.vector.tensor_tensor(
-                    staged[:], banks[j][:], parked[:, j * PIECE : (j + 1) * PIECE], ADD
-                )
-                store(staged, 0, j)
+                dense(banks[j], 0, j, range(SPLIT, DENSE), start=True)
+                finish(banks[j], 0, j)

@@ -14,6 +14,7 @@ PIECES = POINTS // PIECE
 DENSE = 8
 TABLE = DENSE
 STAT = 512
+LOAD = 1024
 EPS = 1e-5
 SPLIT = 4
 
@@ -64,8 +65,8 @@ def tile_decoder_b_kernel(
         for f in (f0, f1, f3):
             for k in range(f.shape[0] // P):
                 block = raws.tile([P, POINTS], F32, name="raw")
-                for c in range(POINTS // STAT):
-                    columns = slice(c * STAT, (c + 1) * STAT)
+                for c in range(POINTS // LOAD):
+                    columns = slice(c * LOAD, (c + 1) * LOAD)
                     nc.sync.dma_start(block[:, columns], f[k * P : (k + 1) * P, columns])
                 if not raw:
                     nc.sync.dma_start(offsets[:], offs)

@@ -14,9 +14,8 @@ PIECES = POINTS // PIECE
 DENSE = 8
 TABLE = DENSE
 STAT = 512
-LOAD = 1024
 EPS = 1e-5
-SPLIT = 4
+SPLIT = 3
 
 FLOPS = 2 * (DENSE + 1) * P * FEATURES * POINTS
 
@@ -65,8 +64,8 @@ def tile_decoder_b_kernel(
         for f in (f0, f1, f3):
             for k in range(f.shape[0] // P):
                 block = raws.tile([P, POINTS], F32, name="raw")
-                for c in range(POINTS // LOAD):
-                    columns = slice(c * LOAD, (c + 1) * LOAD)
+                for c in range(POINTS // STAT):
+                    columns = slice(c * STAT, (c + 1) * STAT)
                     nc.sync.dma_start(block[:, columns], f[k * P : (k + 1) * P, columns])
                 if not raw:
                     nc.sync.dma_start(offsets[:], offs)
@@ -153,53 +152,55 @@ def tile_decoder_b_kernel(
             def open_banks():
                 return [sums.tile([P, PIECE], F32, name="bank") for j in range(PIECES)]
 
-            def gathered(bank, half, j, stop):
+            def gathered(bank, half, j, start):
                 listed = offsets[:, j * (PIECE // 16) : (j + 1) * (PIECE // 16)]
                 nc.tensor.matmul(
                     bank[:], weights[:, TABLE, half * P : (half + 1) * P],
-                    window[:].indirect(listed), start=True, stop=stop,
+                    window[:].indirect(listed), start=start, stop=False,
                 )
 
-            def dense(bank, half, j, blocks, start):
-                for k in blocks:
-                    nc.tensor.matmul(
-                        bank[:], weights[:, k, half * P : (half + 1) * P],
-                        y[k][:, j * PIECE : (j + 1) * PIECE],
-                        start=(start and k == blocks[0]), stop=(k == blocks[-1]),
-                    )
+            def dense(bank, half, j, k, start, stop):
+                nc.tensor.matmul(
+                    bank[:], weights[:, k, half * P : (half + 1) * P],
+                    y[k][:, j * PIECE : (j + 1) * PIECE], start=start, stop=stop,
+                )
 
-            def park(bank, half, j, on_vector):
+            def store(half, j):
                 points = slice(j * PIECE, (j + 1) * PIECE)
-                if on_vector:
-                    nc.vector.tensor_copy(total[half][:, points], bank[:])
-                else:
-                    nc.scalar.copy(total[half][:, points], bank[:])
-
-            def finish(bank, half, j):
-                points = slice(j * PIECE, (j + 1) * PIECE)
-                nc.vector.tensor_tensor(total[half][:, points], bank[:], total[half][:, points], ADD)
                 nc.sync.dma_start(out[half * P : (half + 1) * P, points], total[half][:, points])
 
-            table_banks = open_banks()
-            for j in range(PIECES):
-                gathered(table_banks[j], 1, j, stop=True)
-                park(table_banks[j], 1, j, on_vector=(j % 2 == 1))
+
             banks = open_banks()
             for j in range(PIECES):
-                gathered(banks[j], 0, j, stop=False)
+                gathered(banks[j], 0, j, start=True)
             y = [normalised(k) for k in range(SPLIT)]
             for j in range(PIECES):
-                dense(banks[j], 0, j, range(SPLIT), start=False)
-                park(banks[j], 0, j, on_vector=False)
+                for k in range(SPLIT):
+                    dense(banks[j], 0, j, k, start=False, stop=(k == SPLIT - 1))
+                nc.scalar.copy(total[0][:, j * PIECE : (j + 1) * PIECE], banks[j][:])
 
             for k in range(SPLIT, DENSE):
                 y.append(normalised(k))
             banks = open_banks()
+            for k in range(SPLIT):
+                for j in range(PIECES):
+                    dense(banks[j], 1, j, k, start=(k == 0), stop=False)
             for j in range(PIECES):
-                dense(banks[j], 1, j, range(DENSE), start=True)
-                finish(banks[j], 1, j)
+                gathered(banks[j], 1, j, start=False)
+            for j in range(PIECES):
+                for k in range(SPLIT, DENSE):
+                    dense(banks[j], 1, j, k, start=False, stop=(k == DENSE - 1))
+                points = slice(j * PIECE, (j + 1) * PIECE)
+                if j % 2 == 0:
+                    nc.scalar.copy(total[1][:, points], banks[j][:])
+                else:
+                    nc.vector.tensor_copy(total[1][:, points], banks[j][:])
+                store(1, j)
 
             banks = open_banks()
             for j in range(PIECES):
-                dense(banks[j], 0, j, range(SPLIT, DENSE), start=True)
-                finish(banks[j], 0, j)
+                for k in range(SPLIT, DENSE):
+                    dense(banks[j], 0, j, k, start=(k == SPLIT), stop=(k == DENSE - 1))
+                points = slice(j * PIECE, (j + 1) * PIECE)
+                nc.vector.tensor_tensor(total[0][:, points], banks[j][:], total[0][:, points], ADD)
+                store(0, j)

@@ -106,7 +106,7 @@ def tile_decoder_b_kernel(
                 )
             scale, shift = scale_and_shift(stats, k)
             block = normed.tile([P, POINTS], BF16, name="y")
-            scalar_pieces, vector_pieces = (5, 0) if k < DENSE - 1 else (3, 5)
+            scalar_pieces, vector_pieces = (6, 0) if k < DENSE - 1 else (3, 5)
             for j in range(scalar_pieces + vector_pieces):
                 points = slice(j * PIECE, (j + 1) * PIECE)
                 if j < scalar_pieces:

@@ -2,8 +2,10 @@ import concourse.mybir as mybir
 from concourse.masks import make_identity
 
 F32, BF16, U16 = mybir.dt.float32, mybir.dt.bfloat16, mybir.dt.uint16
-MULT, ADD, POW = mybir.AluOpType.mult, mybir.AluOpType.add, mybir.AluOpType.pow
-IDENTITY = mybir.ActivationFunctionType.Identity
+MULT, ADD = mybir.AluOpType.mult, mybir.AluOpType.add
+IDENTITY, COPY = mybir.ActivationFunctionType.Identity, mybir.ActivationFunctionType.Copy
+SQUARE = mybir.ActivationFunctionType.Square
+RSQRT = mybir.ActivationFunctionType.Abs_reciprocal_sqrt
 
 P = 128
 POINTS = 4096
@@ -12,7 +14,6 @@ FEATURES = 256
 PIECE = 512
 PIECES = POINTS // PIECE
 DENSE = 8
-TABLE = DENSE
 STAT = 512
 EPS = 1e-5
 SPLIT = 3
@@ -25,12 +26,6 @@ def tile_decoder_b_kernel(
     f3, gamma3, beta3, w3, offs, out,
 ):
     nc = tc.nc
-    parameters = (
-        (gamma2, beta2, w2, TABLE),
-        (gamma0, beta0, w0, 0),
-        (gamma1, beta1, w1, 4),
-        (gamma3, beta3, w3, 6),
-    )
 
     with (
         tc.tile_pool(name="held", bufs=1) as held,
@@ -38,64 +33,62 @@ def tile_decoder_b_kernel(
         tc.tile_pool(name="normed", bufs=DENSE) as normed,
         tc.tile_pool(name="small", bufs=4) as small,
     ):
+
+        def load_parameters(gamma, beta, w, level):
+            blocks = w.shape[0] // P
+            gain = held.tile([P, blocks], F32, name=f"gain{level}")
+            nc.sync.dma_start(gain[:], gamma.rearrange("(k c) o -> c (k o)", c=P))
+            bias = held.tile([P, blocks], F32, name=f"bias{level}")
+            nc.sync.dma_start(bias[:], beta.rearrange("(k c) o -> c (k o)", c=P))
+            return gain, bias
+
+        def load_weights(w, level):
+            weights = held.tile([P, w.shape[0] // P, FEATURES], BF16, name=f"weights{level}")
+            nc.sync.dma_start(weights[:], w.rearrange("(k c) m -> c k m", c=P))
+            return weights
+
         table_rows = held.tile([P, COARSE // P, P], BF16, name="table_rows")
         nc.sync.dma_start(table_rows[:], table.rearrange("(g p) d -> p g d", p=P))
-
-        param_rows = held.tile([P, P], F32, name="param_rows")
-        nc.vector.memset(param_rows[:], 0.0)
-        for gamma, beta, w, first in parameters:
-            blocks = w.shape[0] // P
-            nc.scalar.dma_start(
-                param_rows[first : first + blocks, :], gamma.rearrange("(k c) o -> k (c o)", c=P)
-            )
-            nc.scalar.dma_start(
-                param_rows[DENSE + 1 + first : DENSE + 1 + first + blocks, :],
-                beta.rearrange("(k c) o -> k (c o)", c=P),
-            )
-        weights = held.tile([P, DENSE + 1, FEATURES], BF16, name="weights")
-        for gamma, beta, w, first in parameters:
-            nc.scalar.dma_start(
-                weights[:, first : first + w.shape[0] // P, :],
-                w.rearrange("(k c) m -> c k m", c=P),
-            )
-
+        table_gain, table_bias = load_parameters(gamma2, beta2, w2, 2)
         offsets = held.tile([P, POINTS // 16], U16, name="offsets")
+        nc.sync.dma_start(offsets[:], offs)
+        table_weights = load_weights(w2, 2)
+
         raw = []
-        for f in (f0, f1, f3):
+        gain_of, bias_of, weights_of = [], [], []
+        for level, f, gamma, beta, w in (
+            (0, f0, gamma0, beta0, w0), (1, f1, gamma1, beta1, w1), (3, f3, gamma3, beta3, w3)
+        ):
+            gain, bias = load_parameters(gamma, beta, w, level)
             for k in range(f.shape[0] // P):
                 block = raws.tile([P, POINTS], F32, name="raw")
                 for c in range(POINTS // STAT):
                     columns = slice(c * STAT, (c + 1) * STAT)
                     nc.sync.dma_start(block[:, columns], f[k * P : (k + 1) * P, columns])
-                if not raw:
-                    nc.sync.dma_start(offsets[:], offs)
+                if k == 0:
+                    weights = load_weights(w, level)
                 raw.append(block)
+                gain_of.append(gain[:, k : k + 1])
+                bias_of.append(bias[:, k : k + 1])
+                weights_of.append(weights[:, k, :])
 
-        identity_bf16 = held.tile([P, P], BF16, name="identity_bf16")
-        make_identity(nc, identity_bf16[:])
-        identity_f32 = held.tile([P, P], F32, name="identity_f32")
-        make_identity(nc, identity_f32[:])
-        minus_half = held.tile([P, 1], F32, name="minus_half")
-        nc.vector.memset(minus_half[:], -0.5)
+        identity = held.tile([P, P], BF16, name="identity")
+        make_identity(nc, identity[:])
+        eps = held.tile([P, 1], F32, name="eps")
+        nc.vector.memset(eps[:], EPS)
 
-        gain = held.tile([P, DENSE + 1, 2], F32, name="gain")
-        bias = held.tile([P, DENSE + 1], F32, name="bias")
         window = held.tile([P, COARSE], BF16, name="window")
         total = [held.tile([P, POINTS], F32, name=f"total{half}") for half in range(2)]
 
-        def scale_and_shift(stats, k):
-            mean_var = small.tile([P, 2], F32, name="mean_var")
-            nc.vector.bn_aggr(mean_var[:], stats[:])
-            spread = small.tile([P, 1], F32, name="spread")
-            nc.gpsimd.tensor_scalar_add(spread[:], mean_var[:, 1:2], EPS)
+        def scale_and_shift(mean, spread, share, gain, bias):
             rstd = small.tile([P, 1], F32, name="rstd")
-            nc.gpsimd.tensor_tensor(rstd[:], spread[:], minus_half[:], POW)
-            scale = small.tile([P, 2], F32, name="scale")
-            nc.gpsimd.tensor_scalar_mul(scale[:], gain[:, k, :], rstd[:])
+            nc.scalar.activation(rstd[:], spread, RSQRT, bias=eps[:], scale=share)
+            scale = small.tile([P, 1], F32, name="scale")
+            nc.scalar.activation(scale[:], rstd[:], IDENTITY, scale=gain)
+            drop = small.tile([P, 1], F32, name="drop")
+            nc.scalar.activation(drop[:], mean, IDENTITY, scale=scale[:])
             shift = small.tile([P, 1], F32, name="shift")
-            nc.gpsimd.tensor_scalar(
-                shift[:], mean_var[:, 0:1], scale[:, 1:2], bias[:, k : k + 1], MULT, ADD
-            )
+            nc.scalar.activation(shift[:], drop[:], IDENTITY, bias=bias, scale=-1.0)
             return scale, shift
 
         def normalised(k):
@@ -104,48 +97,50 @@ def tile_decoder_b_kernel(
                 nc.vector.bn_stats(
                     stats[:, 6 * c : 6 * c + 6], raw[k][:, c * STAT : (c + 1) * STAT]
                 )
-            scale, shift = scale_and_shift(stats, k)
+            mean_var = small.tile([P, 2], F32, name="mean_var")
+            nc.vector.bn_aggr(mean_var[:], stats[:])
+            scale, shift = scale_and_shift(
+                mean_var[:, 0:1], mean_var[:, 1:2], 1.0, gain_of[k], bias_of[k]
+            )
             block = normed.tile([P, POINTS], BF16, name="y")
-            scalar_pieces, vector_pieces = (6, 0) if k < DENSE - 1 else (3, 5)
+            scalar_pieces, vector_pieces = (4, 0) if k < DENSE - 1 else (3, 5)
             for j in range(scalar_pieces + vector_pieces):
                 points = slice(j * PIECE, (j + 1) * PIECE)
                 if j < scalar_pieces:
                     nc.scalar.activation(
                         block[:, points], raw[k][:, points], IDENTITY,
-                        bias=shift[:], scale=scale[:, 0:1],
+                        bias=shift[:], scale=scale[:],
                     )
                 else:
                     nc.vector.tensor_scalar(
-                        block[:, points], raw[k][:, points], scale[:, 0:1], shift[:], MULT, ADD
+                        block[:, points], raw[k][:, points], scale[:], shift[:], MULT, ADD
                     )
             if scalar_pieces + vector_pieces < PIECES:
                 rest = slice((scalar_pieces + vector_pieces) * PIECE, POINTS)
                 nc.gpsimd.tensor_scalar(
-                    block[:, rest], raw[k][:, rest], scale[:, 0:1], shift[:], MULT, ADD
+                    block[:, rest], raw[k][:, rest], scale[:], shift[:], MULT, ADD
                 )
             return block
 
         with tc.psum_pool(name="flips", bufs=1) as flips:
-            param_columns = flips.tile([P, P], F32, name="param_columns")
-            nc.tensor.transpose(param_columns[:], param_rows[:], identity_f32[:])
-            nc.vector.tensor_copy(gain[:, :, 0], param_columns[:, 0 : DENSE + 1])
-            nc.vector.tensor_scalar_mul(gain[:, :, 1], param_columns[:, 0 : DENSE + 1], -1.0)
-            nc.vector.tensor_copy(bias[:], param_columns[:, DENSE + 1 : 2 * (DENSE + 1)])
-
             flipped = flips.tile([P, COARSE], BF16, name="flipped")
             for g in range(COARSE // P):
                 nc.tensor.transpose(
-                    flipped[:, g * P : (g + 1) * P], table_rows[:, g, :], identity_bf16[:]
+                    flipped[:, g * P : (g + 1) * P], table_rows[:, g, :], identity[:]
                 )
-            table_stats = small.tile([P, 6 * (COARSE // STAT)], F32, name="table_stats")
-            for c in range(COARSE // STAT):
-                nc.vector.bn_stats(
-                    table_stats[:, 6 * c : 6 * c + 6], flipped[:, c * STAT : (c + 1) * STAT]
-                )
-            scale, shift = scale_and_shift(table_stats, TABLE)
+            unused = held.tile([P, COARSE], BF16, name="unused")
+            mean = small.tile([P, 1], F32, name="mean")
             nc.scalar.activation(
-                window[:], flipped[:], IDENTITY, bias=shift[:], scale=scale[:, 0:1]
+                unused[:], flipped[:], COPY, scale=1.0 / COARSE, accum_out=mean[:]
             )
+            spread = small.tile([P, 1], F32, name="spread")
+            nc.scalar.activation(
+                unused[:], flipped[:], SQUARE, bias=mean[:], scale=-1.0, accum_out=spread[:]
+            )
+            scale, shift = scale_and_shift(
+                mean[:], spread[:], 1.0 / COARSE, table_gain[:], table_bias[:]
+            )
+            nc.scalar.activation(window[:], flipped[:], IDENTITY, bias=shift[:], scale=scale[:])
 
         with tc.psum_pool(name="sums", bufs=PIECES) as sums:
 
@@ -155,13 +150,13 @@ def tile_decoder_b_kernel(
             def gathered(bank, half, j, start):
                 listed = offsets[:, j * (PIECE // 16) : (j + 1) * (PIECE // 16)]
                 nc.tensor.matmul(
-                    bank[:], weights[:, TABLE, half * P : (half + 1) * P],
+                    bank[:], table_weights[:, 0, half * P : (half + 1) * P],
                     window[:].indirect(listed), start=start, stop=False,
                 )
 
             def dense(bank, half, j, k, start, stop):
                 nc.tensor.matmul(
-                    bank[:], weights[:, k, half * P : (half + 1) * P],
+                    bank[:], weights_of[k][:, half * P : (half + 1) * P],
                     y[k][:, j * PIECE : (j + 1) * PIECE], start=start, stop=stop,
                 )
 

@@ -16,7 +16,8 @@ PIECES = POINTS // PIECE
 DENSE = 8
 STAT = 512
 EPS = 1e-5
-SPLIT = 3
+FIRST = 3
+SECOND = 5
 
 FLOPS = 2 * (DENSE + 1) * P * FEATURES * POINTS
 
@@ -160,42 +161,49 @@ def tile_decoder_b_kernel(
                     y[k][:, j * PIECE : (j + 1) * PIECE], start=start, stop=stop,
                 )
 
-            def store(half, j):
+            def park(bank, half, j):
+                nc.scalar.copy(total[half][:, j * PIECE : (j + 1) * PIECE], bank[:])
+
+            def finish(bank, half, j):
                 points = slice(j * PIECE, (j + 1) * PIECE)
+                nc.vector.tensor_tensor(
+                    total[half][:, points], bank[:], total[half][:, points], ADD
+                )
                 nc.sync.dma_start(out[half * P : (half + 1) * P, points], total[half][:, points])
 
 
             banks = open_banks()
             for j in range(PIECES):
                 gathered(banks[j], 0, j, start=True)
-            y = [normalised(k) for k in range(SPLIT)]
+            y = [normalised(k) for k in range(FIRST)]
             for j in range(PIECES):
-                for k in range(SPLIT):
-                    dense(banks[j], 0, j, k, start=False, stop=(k == SPLIT - 1))
-                nc.scalar.copy(total[0][:, j * PIECE : (j + 1) * PIECE], banks[j][:])
+                for k in range(FIRST):
+                    dense(banks[j], 0, j, k, start=False, stop=(k == FIRST - 1))
+                park(banks[j], 0, j)
 
-            for k in range(SPLIT, DENSE):
+            for k in range(FIRST, SECOND):
                 y.append(normalised(k))
             banks = open_banks()
-            for k in range(SPLIT):
+            for k in range(FIRST):
                 for j in range(PIECES):
                     dense(banks[j], 1, j, k, start=(k == 0), stop=False)
             for j in range(PIECES):
                 gathered(banks[j], 1, j, start=False)
             for j in range(PIECES):
-                for k in range(SPLIT, DENSE):
-                    dense(banks[j], 1, j, k, start=False, stop=(k == DENSE - 1))
-                points = slice(j * PIECE, (j + 1) * PIECE)
-                if j % 2 == 0:
-                    nc.scalar.copy(total[1][:, points], banks[j][:])
-                else:
-                    nc.vector.tensor_copy(total[1][:, points], banks[j][:])
-                store(1, j)
+                for k in range(FIRST, SECOND):
+                    dense(banks[j], 1, j, k, start=False, stop=(k == SECOND - 1))
+                park(banks[j], 1, j)
+
+            for k in range(SECOND, DENSE):
+                y.append(normalised(k))
+            banks = open_banks()
+            for j in range(PIECES):
+                for k in range(FIRST, DENSE):
+                    dense(banks[j], 0, j, k, start=(k == FIRST), stop=(k == DENSE - 1))
+                finish(banks[j], 0, j)
 
             banks = open_banks()
             for j in range(PIECES):
-                for k in range(SPLIT, DENSE):
-                    dense(banks[j], 0, j, k, start=(k == SPLIT), stop=(k == DENSE - 1))
-                points = slice(j * PIECE, (j + 1) * PIECE)
-                nc.vector.tensor_tensor(total[0][:, points], banks[j][:], total[0][:, points], ADD)
-                store(0, j)
+                for k in range(SECOND, DENSE):
+                    dense(banks[j], 1, j, k, start=(k == SECOND), stop=(k == DENSE - 1))
+                finish(banks[j], 1, j)

@@ -104,23 +104,13 @@ def tile_decoder_b_kernel(
                 mean_var[:, 0:1], mean_var[:, 1:2], 1.0, gain_of[k], bias_of[k]
             )
             block = normed.tile([P, POINTS], BF16, name="y")
-            scalar_pieces, vector_pieces = (4, 0) if k < DENSE - 1 else (3, 5)
-            for j in range(scalar_pieces + vector_pieces):
+            for j in range(PIECES // 2):
                 points = slice(j * PIECE, (j + 1) * PIECE)
-                if j < scalar_pieces:
-                    nc.scalar.activation(
-                        block[:, points], raw[k][:, points], IDENTITY,
-                        bias=shift[:], scale=scale[:],
-                    )
-                else:
-                    nc.vector.tensor_scalar(
-                        block[:, points], raw[k][:, points], scale[:], shift[:], MULT, ADD
-                    )
-            if scalar_pieces + vector_pieces < PIECES:
-                rest = slice((scalar_pieces + vector_pieces) * PIECE, POINTS)
-                nc.gpsimd.tensor_scalar(
-                    block[:, rest], raw[k][:, rest], scale[:], shift[:], MULT, ADD
+                nc.scalar.activation(
+                    block[:, points], raw[k][:, points], IDENTITY, bias=shift[:], scale=scale[:]
                 )
+            rest = slice(POINTS // 2, POINTS)
+            nc.gpsimd.tensor_scalar(block[:, rest], raw[k][:, rest], scale[:], shift[:], MULT, ADD)
             return block
 
         with tc.psum_pool(name="flips", bufs=1) as flips:

@@ -16,7 +16,7 @@ PIECES = POINTS // PIECE
 DENSE = 8
 STAT = 512
 EPS = 1e-5
-FIRST = 3
+FIRST = 2
 SECOND = 5
 
 FLOPS = 2 * (DENSE + 1) * P * FEATURES * POINTS

@@ -63,8 +63,9 @@ def tile_decoder_b_kernel(
             gain, bias = load_parameters(gamma, beta, w, level)
             for k in range(f.shape[0] // P):
                 block = raws.tile([P, POINTS], F32, name="raw")
-                for c in range(POINTS // STAT):
-                    columns = slice(c * STAT, (c + 1) * STAT)
+                width = STAT if len(raw) == DENSE - 1 else 2 * STAT
+                for first in range(0, POINTS, width):
+                    columns = slice(first, first + width)
                     nc.sync.dma_start(block[:, columns], f[k * P : (k + 1) * P, columns])
                 if k == 0:
                     weights = load_weights(w, level)

@@ -82,15 +82,13 @@ def tile_decoder_b_kernel(
         window = held.tile([P, COARSE], BF16, name="window")
         total = [held.tile([P, POINTS], F32, name=f"total{half}") for half in range(2)]
 
-        def scale_and_shift(mean, spread, share, gain, bias):
+        def scale_and_shift(minus_mean, spread, share, gain, bias):
             rstd = small.tile([P, 1], F32, name="rstd")
             nc.scalar.activation(rstd[:], spread, RSQRT, bias=eps[:], scale=share)
             scale = small.tile([P, 1], F32, name="scale")
             nc.scalar.activation(scale[:], rstd[:], IDENTITY, scale=gain)
-            drop = small.tile([P, 1], F32, name="drop")
-            nc.scalar.activation(drop[:], mean, IDENTITY, scale=scale[:])
             shift = small.tile([P, 1], F32, name="shift")
-            nc.scalar.activation(shift[:], drop[:], IDENTITY, bias=bias, scale=-1.0)
+            nc.scalar.activation(shift[:], scale[:], IDENTITY, bias=bias, scale=minus_mean)
             return scale, shift
 
         def normalised(k):
@@ -101,8 +99,10 @@ def tile_decoder_b_kernel(
                 )
             mean_var = small.tile([P, 2], F32, name="mean_var")
             nc.vector.bn_aggr(mean_var[:], stats[:])
+            minus_mean = small.tile([P, 1], F32, name="minus_mean")
+            nc.vector.tensor_scalar_mul(minus_mean[:], mean_var[:, 0:1], -1.0)
             scale, shift = scale_and_shift(
-                mean_var[:, 0:1], mean_var[:, 1:2], 1.0, gain_of[k], bias_of[k]
+                minus_mean[:], mean_var[:, 1:2], 1.0, gain_of[k], bias_of[k]
             )
             block = normed.tile([P, POINTS], BF16, name="y")
             for j in range(PIECES // 2):
@@ -121,16 +121,16 @@ def tile_decoder_b_kernel(
                     flipped[:, g * P : (g + 1) * P], table_rows[:, g, :], identity[:]
                 )
             unused = held.tile([P, COARSE], BF16, name="unused")
-            mean = small.tile([P, 1], F32, name="mean")
+            minus_mean = small.tile([P, 1], F32, name="minus_mean")
             nc.scalar.activation(
-                unused[:], flipped[:], COPY, scale=1.0 / COARSE, accum_out=mean[:]
+                unused[:], flipped[:], COPY, scale=-1.0 / COARSE, accum_out=minus_mean[:]
             )
             spread = small.tile([P, 1], F32, name="spread")
             nc.scalar.activation(
-                unused[:], flipped[:], SQUARE, bias=mean[:], scale=-1.0, accum_out=spread[:]
+                unused[:], flipped[:], SQUARE, bias=minus_mean[:], accum_out=spread[:]
             )
             scale, shift = scale_and_shift(
-                mean[:], spread[:], 1.0 / COARSE, table_gain[:], table_bias[:]
+                minus_mean[:], spread[:], 1.0 / COARSE, table_gain[:], table_bias[:]
             )
             nc.scalar.activation(window[:], flipped[:], IDENTITY, bias=shift[:], scale=scale[:])
 

@@ -63,7 +63,7 @@ def tile_decoder_b_kernel(
             gain, bias = load_parameters(gamma, beta, w, level)
             for k in range(f.shape[0] // P):
                 block = raws.tile([P, POINTS], F32, name="raw")
-                width = STAT if len(raw) == DENSE - 1 else 2 * STAT
+                width = {0: 2 * STAT, 1: 2 * STAT, DENSE - 1: STAT}.get(len(raw), 4 * STAT)
                 for first in range(0, POINTS, width):
                     columns = slice(first, first + width)
                     nc.sync.dma_start(block[:, columns], f[k * P : (k + 1) * P, columns])

@@ -13,6 +13,7 @@ COARSE = 1024
 FEATURES = 256
 PIECE = 512
 PIECES = POINTS // PIECE
+NEAR, FAR = range(PIECES // 2), range(PIECES // 2, PIECES)
 DENSE = 8
 STAT = 512
 EPS = 1e-5
@@ -38,18 +39,18 @@ def tile_decoder_b_kernel(
         def load_parameters(gamma, beta, w, level):
             blocks = w.shape[0] // P
             gain = held.tile([P, blocks], F32, name=f"gain{level}")
-            nc.sync.dma_start(gain[:], gamma.rearrange("(k c) o -> c (k o)", c=P))
+            nc.sync.dma_start(gain[:], gamma.rearrange("(c k) o -> c (k o)", c=P))
             bias = held.tile([P, blocks], F32, name=f"bias{level}")
-            nc.sync.dma_start(bias[:], beta.rearrange("(k c) o -> c (k o)", c=P))
+            nc.sync.dma_start(bias[:], beta.rearrange("(c k) o -> c (k o)", c=P))
             return gain, bias
 
         def load_weights(w, level):
             weights = held.tile([P, w.shape[0] // P, FEATURES], BF16, name=f"weights{level}")
-            nc.sync.dma_start(weights[:], w.rearrange("(k c) m -> c k m", c=P))
+            nc.sync.dma_start(weights[:], w.rearrange("(c k) m -> c k m", c=P))
             return weights
 
         table_rows = held.tile([P, COARSE // P, P], BF16, name="table_rows")
-        nc.sync.dma_start(table_rows[:], table.rearrange("(g p) d -> p g d", p=P))
+        nc.sync.dma_start(table_rows[:], table.rearrange("(p g) d -> p g d", p=P))
         table_gain, table_bias = load_parameters(gamma2, beta2, w2, 2)
         offsets = held.tile([P, POINTS // 16], U16, name="offsets")
         nc.sync.dma_start(offsets[:], offs)
@@ -61,12 +62,13 @@ def tile_decoder_b_kernel(
             (0, f0, gamma0, beta0, w0), (1, f1, gamma1, beta1, w1), (3, f3, gamma3, beta3, w3)
         ):
             gain, bias = load_parameters(gamma, beta, w, level)
+            channels = f.rearrange("(c k) n -> k c n", c=P)
             for k in range(f.shape[0] // P):
                 block = raws.tile([P, POINTS], F32, name="raw")
                 width = {0: 2 * STAT, 1: 2 * STAT, DENSE - 1: STAT}.get(len(raw), 4 * STAT)
                 for first in range(0, POINTS, width):
                     columns = slice(first, first + width)
-                    nc.sync.dma_start(block[:, columns], f[k * P : (k + 1) * P, columns])
+                    nc.sync.dma_start(block[:, columns], channels[k, :, columns])
                 if k == 0:
                     weights = load_weights(w, level)
                 raw.append(block)
@@ -105,7 +107,7 @@ def tile_decoder_b_kernel(
                 minus_mean[:], mean_var[:, 1:2], 1.0, gain_of[k], bias_of[k]
             )
             block = normed.tile([P, POINTS], BF16, name="y")
-            for j in range(PIECES // 2):
+            for j in NEAR:
                 points = slice(j * PIECE, (j + 1) * PIECE)
                 nc.scalar.activation(
                     block[:, points], raw[k][:, points], IDENTITY, bias=shift[:], scale=scale[:]
@@ -132,12 +134,19 @@ def tile_decoder_b_kernel(
             scale, shift = scale_and_shift(
                 minus_mean[:], spread[:], 1.0 / COARSE, table_gain[:], table_bias[:]
             )
-            nc.scalar.activation(window[:], flipped[:], IDENTITY, bias=shift[:], scale=scale[:])
+            nc.scalar.activation(
+                window[:].rearrange("d (p g) -> d p g", p=P),
+                flipped[:].rearrange("d (g p) -> d p g", p=P),
+                IDENTITY, bias=shift[:], scale=scale[:],
+            )
 
         with tc.psum_pool(name="sums", bufs=PIECES) as sums:
 
-            def open_banks():
-                return [sums.tile([P, PIECE], F32, name="bank") for j in range(PIECES)]
+            def open_banks(pieces):
+                return [
+                    (sums.tile([P, PIECE], F32, name="bank"), half, j)
+                    for j in pieces for half in range(2)
+                ]
 
             def gathered(bank, half, j, start):
                 listed = offsets[:, j * (PIECE // 16) : (j + 1) * (PIECE // 16)]
@@ -163,38 +172,38 @@ def tile_decoder_b_kernel(
                 nc.sync.dma_start(out[half * P : (half + 1) * P, points], total[half][:, points])
 
 
-            banks = open_banks()
-            for j in range(PIECES):
-                gathered(banks[j], 0, j, start=True)
+            banks = open_banks(NEAR)
+            for bank, half, j in banks:
+                gathered(bank, half, j, start=True)
             y = [normalised(k) for k in range(FIRST)]
-            for j in range(PIECES):
+            for bank, half, j in banks:
                 for k in range(FIRST):
-                    dense(banks[j], 0, j, k, start=False, stop=(k == FIRST - 1))
-                park(banks[j], 0, j)
+                    dense(bank, half, j, k, start=False, stop=(k == FIRST - 1))
+                park(bank, half, j)
 
             for k in range(FIRST, SECOND):
                 y.append(normalised(k))
-            banks = open_banks()
+            banks = open_banks(FAR)
             for k in range(FIRST):
-                for j in range(PIECES):
-                    dense(banks[j], 1, j, k, start=(k == 0), stop=False)
-            for j in range(PIECES):
-                gathered(banks[j], 1, j, start=False)
-            for j in range(PIECES):
+                for bank, half, j in banks:
+                    dense(bank, half, j, k, start=(k == 0), stop=False)
+            for bank, half, j in banks:
+                gathered(bank, half, j, start=False)
+            for bank, half, j in banks:
                 for k in range(FIRST, SECOND):
-                    dense(banks[j], 1, j, k, start=False, stop=(k == SECOND - 1))
-                park(banks[j], 1, j)
+                    dense(bank, half, j, k, start=False, stop=(k == SECOND - 1))
+                park(bank, half, j)
 
             for k in range(SECOND, DENSE):
                 y.append(normalised(k))
-            banks = open_banks()
-            for j in range(PIECES):
+            banks = open_banks(NEAR)
+            for bank, half, j in banks:
                 for k in range(FIRST, DENSE):
-                    dense(banks[j], 0, j, k, start=(k == FIRST), stop=(k == DENSE - 1))
-                finish(banks[j], 0, j)
+                    dense(bank, half, j, k, start=(k == FIRST), stop=(k == DENSE - 1))
+                finish(bank, half, j)
 
-            banks = open_banks()
-            for j in range(PIECES):
+            banks = open_banks(FAR)
+            for bank, half, j in banks:
                 for k in range(SECOND, DENSE):
-                    dense(banks[j], 1, j, k, start=(k == SECOND), stop=(k == DENSE - 1))
-                finish(banks[j], 1, j)
+                    dense(bank, half, j, k, start=(k == SECOND), stop=(k == DENSE - 1))
+                finish(bank, half, j)

@@ -31,7 +31,7 @@ def tile_decoder_b_kernel(
 
     with (
         tc.tile_pool(name="held", bufs=1) as held,
-        tc.tile_pool(name="raws", bufs=DENSE) as raws,
+        tc.tile_pool(name="raws", bufs=DENSE - 1) as raws,
         tc.tile_pool(name="normed", bufs=DENSE) as normed,
         tc.tile_pool(name="small", bufs=4) as small,
     ):
@@ -171,6 +171,15 @@ def tile_decoder_b_kernel(
                 )
                 nc.sync.dma_start(out[half * P : (half + 1) * P, points], total[half][:, points])
 
+            def finish_by_others(bank, half, j):
+                points = slice(j * PIECE, (j + 1) * PIECE)
+                late = small.tile([P, PIECE], F32, name="late")
+                nc.scalar.copy(late[:], bank[:])
+                nc.gpsimd.tensor_tensor(
+                    total[half][:, points], late[:], total[half][:, points], ADD
+                )
+                nc.sync.dma_start(out[half * P : (half + 1) * P, points], total[half][:, points])
+
 
             banks = open_banks(NEAR)
             for bank, half, j in banks:
@@ -206,4 +215,7 @@ def tile_decoder_b_kernel(
             for bank, half, j in banks:
                 for k in range(SECOND, DENSE):
                     dense(bank, half, j, k, start=(k == SECOND), stop=(k == DENSE - 1))
-                finish(bank, half, j)
+                if half == 1 and j in FAR[:2]:
+                    finish_by_others(bank, half, j)
+                else:
+                    finish(bank, half, j)

@@ -34,6 +34,7 @@ def tile_decoder_b_kernel(
         tc.tile_pool(name="raws", bufs=DENSE - 1) as raws,
         tc.tile_pool(name="normed", bufs=DENSE) as normed,
         tc.tile_pool(name="small", bufs=4) as small,
+        tc.tile_pool(name="scales", bufs=1) as scales,
     ):
 
         def load_parameters(gamma, beta, w, level):
@@ -80,17 +81,18 @@ def tile_decoder_b_kernel(
         make_identity(nc, identity[:])
         eps = held.tile([P, 1], F32, name="eps")
         nc.vector.memset(eps[:], EPS)
+        first_use = held.tile([P, 1], F32, name="first_use")
+        nc.scalar.activation(first_use[:], eps[:], RSQRT)
 
         window = held.tile([P, COARSE], BF16, name="window")
         total = [held.tile([P, POINTS], F32, name=f"total{half}") for half in range(2)]
 
         def scale_and_shift(minus_mean, spread, share, gain, bias):
-            rstd = small.tile([P, 1], F32, name="rstd")
-            nc.scalar.activation(rstd[:], spread, RSQRT, bias=eps[:], scale=share)
-            scale = small.tile([P, 1], F32, name="scale")
-            nc.scalar.activation(scale[:], rstd[:], IDENTITY, scale=gain)
-            shift = small.tile([P, 1], F32, name="shift")
-            nc.scalar.activation(shift[:], scale[:], IDENTITY, bias=bias, scale=minus_mean)
+            columns = scales.tile([P, 3], F32, name="columns")
+            rstd, scale, shift = (columns[:, i : i + 1] for i in range(3))
+            nc.scalar.activation(rstd, spread, RSQRT, bias=eps[:], scale=share)
+            nc.scalar.activation(scale, rstd, IDENTITY, scale=gain)
+            nc.scalar.activation(shift, scale, IDENTITY, bias=bias, scale=minus_mean)
             return scale, shift
 
         def normalised(k):
@@ -110,10 +112,10 @@ def tile_decoder_b_kernel(
             for j in NEAR:
                 points = slice(j * PIECE, (j + 1) * PIECE)
                 nc.scalar.activation(
-                    block[:, points], raw[k][:, points], IDENTITY, bias=shift[:], scale=scale[:]
+                    block[:, points], raw[k][:, points], IDENTITY, bias=shift, scale=scale
                 )
             rest = slice(POINTS // 2, POINTS)
-            nc.gpsimd.tensor_scalar(block[:, rest], raw[k][:, rest], scale[:], shift[:], MULT, ADD)
+            nc.gpsimd.tensor_scalar(block[:, rest], raw[k][:, rest], scale, shift, MULT, ADD)
             return block
 
         with tc.psum_pool(name="flips", bufs=1) as flips:
@@ -137,7 +139,7 @@ def tile_decoder_b_kernel(
             nc.scalar.activation(
                 window[:].rearrange("d (p g) -> d p g", p=P),
                 flipped[:].rearrange("d (g p) -> d p g", p=P),
-                IDENTITY, bias=shift[:], scale=scale[:],
+                IDENTITY, bias=shift, scale=scale,
             )
 
         with tc.psum_pool(name="sums", bufs=PIECES) as sums:

@@ -16,6 +16,7 @@ PIECES = POINTS // PIECE
 NEAR, FAR = range(PIECES // 2), range(PIECES // 2, PIECES)
 DENSE = 8
 STAT = 512
+CHUNKS = POINTS // STAT
 EPS = 1e-5
 FIRST = 2
 SECOND = 5
@@ -53,9 +54,6 @@ def tile_decoder_b_kernel(
         table_rows = held.tile([P, COARSE // P, P], BF16, name="table_rows")
         nc.sync.dma_start(table_rows[:], table.rearrange("(p g) d -> p g d", p=P))
         table_gain, table_bias = load_parameters(gamma2, beta2, w2, 2)
-        offsets = held.tile([P, POINTS // 16], U16, name="offsets")
-        nc.sync.dma_start(offsets[:], offs)
-        table_weights = load_weights(w2, 2)
 
         raw = []
         gain_of, bias_of, weights_of = [], [], []
@@ -66,10 +64,14 @@ def tile_decoder_b_kernel(
             channels = f.rearrange("(c k) n -> k c n", c=P)
             for k in range(f.shape[0] // P):
                 block = raws.tile([P, POINTS], F32, name="raw")
-                width = {0: 2 * STAT, 1: 2 * STAT, DENSE - 1: STAT}.get(len(raw), 4 * STAT)
+                width = {0: STAT, 1: 2 * STAT, DENSE - 1: STAT}.get(len(raw), 4 * STAT)
                 for first in range(0, POINTS, width):
                     columns = slice(first, first + width)
                     nc.sync.dma_start(block[:, columns], channels[k, :, columns])
+                if not raw:
+                    offsets = held.tile([P, POINTS // 16], U16, name="offsets")
+                    nc.sync.dma_start(offsets[:], offs)
+                    table_weights = load_weights(w2, 2)
                 if k == 0:
                     weights = load_weights(w, level)
                 raw.append(block)
@@ -95,26 +97,33 @@ def tile_decoder_b_kernel(
             nc.scalar.activation(shift, scale, IDENTITY, bias=bias, scale=minus_mean)
             return scale, shift
 
+        stats = [held.tile([P, 6 * CHUNKS], F32, name=f"stats{k}") for k in range(DENSE)]
+
+        def chunk_statistics(k, c):
+            nc.vector.bn_stats(
+                stats[k][:, 6 * c : 6 * c + 6], raw[k][:, c * STAT : (c + 1) * STAT]
+            )
+
         def normalised(k):
-            stats = small.tile([P, 6 * (POINTS // STAT)], F32, name="stats")
-            for c in range(POINTS // STAT):
-                nc.vector.bn_stats(
-                    stats[:, 6 * c : 6 * c + 6], raw[k][:, c * STAT : (c + 1) * STAT]
-                )
+            for c in range(0 if k == 0 else 1, CHUNKS):
+                chunk_statistics(k, c)
+            if k + 1 < DENSE:
+                chunk_statistics(k + 1, 0)
             mean_var = small.tile([P, 2], F32, name="mean_var")
-            nc.vector.bn_aggr(mean_var[:], stats[:])
+            nc.vector.bn_aggr(mean_var[:], stats[k][:])
             minus_mean = small.tile([P, 1], F32, name="minus_mean")
-            nc.vector.tensor_scalar_mul(minus_mean[:], mean_var[:, 0:1], -1.0)
+            nc.gpsimd.tensor_scalar_mul(minus_mean[:], mean_var[:, 0:1], -1.0)
             scale, shift = scale_and_shift(
                 minus_mean[:], mean_var[:, 1:2], 1.0, gain_of[k], bias_of[k]
             )
             block = normed.tile([P, POINTS], BF16, name="y")
-            for j in NEAR:
+            first, second = (FAR, NEAR) if FIRST <= k < SECOND else (NEAR, FAR)
+            for j in first:
                 points = slice(j * PIECE, (j + 1) * PIECE)
                 nc.scalar.activation(
                     block[:, points], raw[k][:, points], IDENTITY, bias=shift, scale=scale
                 )
-            rest = slice(POINTS // 2, POINTS)
+            rest = slice(second[0] * PIECE, (second[-1] + 1) * PIECE)
             nc.gpsimd.tensor_scalar(block[:, rest], raw[k][:, rest], scale, shift, MULT, ADD)
             return block
 

@@ -89,12 +89,13 @@ def tile_decoder_b_kernel(
         window = held.tile([P, COARSE], BF16, name="window")
         total = [held.tile([P, POINTS], F32, name=f"total{half}") for half in range(2)]
 
-        def scale_and_shift(minus_mean, spread, share, gain, bias):
-            columns = scales.tile([P, 3], F32, name="columns")
-            rstd, scale, shift = (columns[:, i : i + 1] for i in range(3))
+        def scale_and_shift(mean, spread, share, gain, minus_gain, bias, slot):
+            columns = scales.tile([P, 4], F32, name=slot)
+            minus_mean_gain, rstd, scale, shift = (columns[:, i : i + 1] for i in range(4))
             nc.scalar.activation(rstd, spread, RSQRT, bias=eps[:], scale=share)
+            nc.scalar.activation(minus_mean_gain, mean, IDENTITY, scale=minus_gain)
+            nc.scalar.activation(shift, rstd, IDENTITY, bias=bias, scale=minus_mean_gain)
             nc.scalar.activation(scale, rstd, IDENTITY, scale=gain)
-            nc.scalar.activation(shift, scale, IDENTITY, bias=bias, scale=minus_mean)
             return scale, shift
 
         stats = [held.tile([P, 6 * CHUNKS], F32, name=f"stats{k}") for k in range(DENSE)]
@@ -105,26 +106,32 @@ def tile_decoder_b_kernel(
             )
 
         def normalised(k):
+            minus_gain = small.tile([P, 1], F32, name="minus_gain")
+            nc.vector.tensor_scalar_mul(minus_gain[:], gain_of[k], -1.0)
             for c in range(0 if k == 0 else 1, CHUNKS):
                 chunk_statistics(k, c)
             if k + 1 < DENSE:
                 chunk_statistics(k + 1, 0)
             mean_var = small.tile([P, 2], F32, name="mean_var")
             nc.vector.bn_aggr(mean_var[:], stats[k][:])
-            minus_mean = small.tile([P, 1], F32, name="minus_mean")
-            nc.gpsimd.tensor_scalar_mul(minus_mean[:], mean_var[:, 0:1], -1.0)
             scale, shift = scale_and_shift(
-                minus_mean[:], mean_var[:, 1:2], 1.0, gain_of[k], bias_of[k]
+                mean_var[:, 0:1], mean_var[:, 1:2], 1.0, gain_of[k], minus_gain[:], bias_of[k],
+                slot="first_columns" if k == 0 else f"columns{k}",
             )
             block = normed.tile([P, POINTS], BF16, name="y")
-            first, second = (FAR, NEAR) if FIRST <= k < SECOND else (NEAR, FAR)
-            for j in first:
+            by_scalar, by_gpsimd = (FAR, [NEAR]) if FIRST <= k < SECOND else (NEAR, [FAR])
+            if k == SECOND:
+                by_scalar, by_gpsimd = [], [NEAR, FAR]
+            for j in by_scalar:
                 points = slice(j * PIECE, (j + 1) * PIECE)
                 nc.scalar.activation(
                     block[:, points], raw[k][:, points], IDENTITY, bias=shift, scale=scale
                 )
-            rest = slice(second[0] * PIECE, (second[-1] + 1) * PIECE)
-            nc.gpsimd.tensor_scalar(block[:, rest], raw[k][:, rest], scale, shift, MULT, ADD)
+            for pieces in by_gpsimd:
+                points = slice(pieces[0] * PIECE, (pieces[-1] + 1) * PIECE)
+                nc.gpsimd.tensor_scalar(
+                    block[:, points], raw[k][:, points], scale, shift, MULT, ADD
+                )
             return block
 
         with tc.psum_pool(name="flips", bufs=1) as flips:
@@ -134,16 +141,19 @@ def tile_decoder_b_kernel(
                     flipped[:, g * P : (g + 1) * P], table_rows[:, g, :], identity[:]
                 )
             unused = held.tile([P, COARSE], BF16, name="unused")
-            minus_mean = small.tile([P, 1], F32, name="minus_mean")
+            mean = small.tile([P, 1], F32, name="mean")
             nc.scalar.activation(
-                unused[:], flipped[:], COPY, scale=-1.0 / COARSE, accum_out=minus_mean[:]
+                unused[:], flipped[:], COPY, scale=1.0 / COARSE, accum_out=mean[:]
             )
             spread = small.tile([P, 1], F32, name="spread")
             nc.scalar.activation(
-                unused[:], flipped[:], SQUARE, bias=minus_mean[:], accum_out=spread[:]
+                unused[:], flipped[:], SQUARE, bias=mean[:], scale=-1.0, accum_out=spread[:]
             )
+            minus_gain = small.tile([P, 1], F32, name="minus_gain")
+            nc.vector.tensor_scalar_mul(minus_gain[:], table_gain[:], -1.0)
             scale, shift = scale_and_shift(
-                minus_mean[:], spread[:], 1.0 / COARSE, table_gain[:], table_bias[:]
+                mean[:], spread[:], 1.0 / COARSE, table_gain[:], minus_gain[:], table_bias[:],
+                slot="first_columns",
             )
             nc.scalar.activation(
                 window[:].rearrange("d (p g) -> d p g", p=P),
@@ -213,8 +223,10 @@ def tile_decoder_b_kernel(
                 for k in range(FIRST, SECOND):
                     dense(bank, half, j, k, start=False, stop=(k == SECOND - 1))
                 park(bank, half, j)
+                if (half, j) == (1, FAR[1]):
+                    y.append(normalised(SECOND))
 
-            for k in range(SECOND, DENSE):
+            for k in range(SECOND + 1, DENSE):
                 y.append(normalised(k))
             banks = open_banks(NEAR)
             for bank, half, j in banks:

@@ -64,10 +64,12 @@ def tile_decoder_b_kernel(
             channels = f.rearrange("(c k) n -> k c n", c=P)
             for k in range(f.shape[0] // P):
                 block = raws.tile([P, POINTS], F32, name="raw")
-                width = {0: STAT, 1: 2 * STAT, DENSE - 1: STAT}.get(len(raw), 4 * STAT)
-                for first in range(0, POINTS, width):
-                    columns = slice(first, first + width)
-                    nc.sync.dma_start(block[:, columns], channels[k, :, columns])
+                width = (2 if len(raw) in (0, 1, DENSE - 1) else 4) * STAT
+                starts = list(range(0, POINTS, width))
+                if len(raw) == DENSE - 1:
+                    starts.append(POINTS - width // 2)
+                for first, end in zip(starts, starts[1:] + [POINTS]):
+                    nc.sync.dma_start(block[:, first:end], channels[k, :, first:end])
                 if not raw:
                     offsets = held.tile([P, POINTS // 16], U16, name="offsets")
                     nc.sync.dma_start(offsets[:], offs)
@@ -199,7 +201,7 @@ def tile_decoder_b_kernel(
                 nc.gpsimd.tensor_tensor(
                     total[half][:, points], late[:], total[half][:, points], ADD
                 )
-                nc.sync.dma_start(out[half * P : (half + 1) * P, points], total[half][:, points])
+                nc.scalar.dma_start(out[half * P : (half + 1) * P, points], total[half][:, points])
 
 
             banks = open_banks(NEAR)

@@ -102,20 +102,36 @@ def tile_decoder_b_kernel(
 
         stats = [held.tile([P, 6 * CHUNKS], F32, name=f"stats{k}") for k in range(DENSE)]
 
+        unused = held.tile([P, COARSE], BF16, name="unused")
+
         def chunk_statistics(k, c):
             nc.vector.bn_stats(
                 stats[k][:, 6 * c : 6 * c + 6], raw[k][:, c * STAT : (c + 1) * STAT]
             )
 
+        def first_chunk_by_scalar(k):
+            chunk = raw[k][:, :STAT]
+            mean, squares = stats[k][:, 4:5], stats[k][:, 5:6]
+            nc.scalar.activation(unused[:, :STAT], chunk, COPY, scale=1.0 / STAT, accum_out=mean)
+            nc.scalar.activation(
+                unused[:, :STAT], chunk, SQUARE, bias=mean, scale=-1.0, accum_out=squares
+            )
+
+        shared = range(SECOND + 1, DENSE)
+        for k in shared:
+            nc.vector.memset(stats[k][:, 3:4], STAT)
+
         def normalised(k):
             minus_gain = small.tile([P, 1], F32, name="minus_gain")
             nc.vector.tensor_scalar_mul(minus_gain[:], gain_of[k], -1.0)
-            for c in range(0 if k == 0 else 1, CHUNKS):
+            if k == 0:
+                chunk_statistics(0, 0)
+            for c in range(2 if k in shared else 1, CHUNKS):
                 chunk_statistics(k, c)
             if k + 1 < DENSE:
-                chunk_statistics(k + 1, 0)
+                chunk_statistics(k + 1, 1 if k + 1 in shared else 0)
             mean_var = small.tile([P, 2], F32, name="mean_var")
-            nc.vector.bn_aggr(mean_var[:], stats[k][:])
+            nc.vector.bn_aggr(mean_var[:], stats[k][:, 3 if k in shared else 0 :])
             scale, shift = scale_and_shift(
                 mean_var[:, 0:1], mean_var[:, 1:2], 1.0, gain_of[k], minus_gain[:], bias_of[k],
                 slot="first_columns" if k == 0 else f"columns{k}",
@@ -124,6 +140,9 @@ def tile_decoder_b_kernel(
             by_scalar, by_gpsimd = (FAR, [NEAR]) if FIRST <= k < SECOND else (NEAR, [FAR])
             if k == SECOND:
                 by_scalar, by_gpsimd = [], [NEAR, FAR]
+            elif k == DENSE - 1:
+                by_scalar = [*NEAR[:2], *FAR[:2]]
+                by_gpsimd = [NEAR[2:], FAR[2:]]
             for j in by_scalar:
                 points = slice(j * PIECE, (j + 1) * PIECE)
                 nc.scalar.activation(
@@ -142,7 +161,6 @@ def tile_decoder_b_kernel(
                 nc.tensor.transpose(
                     flipped[:, g * P : (g + 1) * P], table_rows[:, g, :], identity[:]
                 )
-            unused = held.tile([P, COARSE], BF16, name="unused")
             mean = small.tile([P, 1], F32, name="mean")
             nc.scalar.activation(
                 unused[:], flipped[:], COPY, scale=1.0 / COARSE, accum_out=mean[:]
@@ -228,7 +246,8 @@ def tile_decoder_b_kernel(
                 if (half, j) == (1, FAR[1]):
                     y.append(normalised(SECOND))
 
-            for k in range(SECOND + 1, DENSE):
+            for k in shared:
+                first_chunk_by_scalar(k)
                 y.append(normalised(k))
             banks = open_banks(NEAR)
             for bank, half, j in banks:

import concourse.mybir as mybir
from concourse.masks import make_identity

F32, BF16, U16 = mybir.dt.float32, mybir.dt.bfloat16, mybir.dt.uint16
MULT, ADD = mybir.AluOpType.mult, mybir.AluOpType.add
IDENTITY, COPY = mybir.ActivationFunctionType.Identity, mybir.ActivationFunctionType.Copy
SQUARE = mybir.ActivationFunctionType.Square
RSQRT = mybir.ActivationFunctionType.Abs_reciprocal_sqrt

P = 128
POINTS = 4096
COARSE = 1024
FEATURES = 256
PIECE = 512
PIECES = POINTS // PIECE
NEAR, FAR = range(PIECES // 2), range(PIECES // 2, PIECES)
DENSE = 8
STAT = 512
CHUNKS = POINTS // STAT
EPS = 1e-5
FIRST = 2
SECOND = 5

FLOPS = 2 * (DENSE + 1) * P * FEATURES * POINTS


def tile_decoder_b_kernel(
    tc, f0, gamma0, beta0, w0, f1, gamma1, beta1, w1, table, gamma2, beta2, w2,
    f3, gamma3, beta3, w3, offs, out,
):
    nc = tc.nc

    with (
        tc.tile_pool(name="held", bufs=1) as held,
        tc.tile_pool(name="raws", bufs=DENSE - 1) as raws,
        tc.tile_pool(name="normed", bufs=DENSE) as normed,
        tc.tile_pool(name="small", bufs=4) as small,
        tc.tile_pool(name="scales", bufs=1) as scales,
    ):

        def load_parameters(gamma, beta, w, level):
            blocks = w.shape[0] // P
            gain = held.tile([P, blocks], F32, name=f"gain{level}")
            nc.sync.dma_start(gain[:], gamma.rearrange("(c k) o -> c (k o)", c=P))
            bias = held.tile([P, blocks], F32, name=f"bias{level}")
            nc.sync.dma_start(bias[:], beta.rearrange("(c k) o -> c (k o)", c=P))
            return gain, bias

        def load_weights(w, level):
            weights = held.tile([P, w.shape[0] // P, FEATURES], BF16, name=f"weights{level}")
            nc.sync.dma_start(weights[:], w.rearrange("(c k) m -> c k m", c=P))
            return weights

        table_rows = held.tile([P, COARSE // P, P], BF16, name="table_rows")
        nc.sync.dma_start(table_rows[:], table.rearrange("(p g) d -> p g d", p=P))
        table_gain, table_bias = load_parameters(gamma2, beta2, w2, 2)

        raw = []
        gain_of, bias_of, weights_of = [], [], []
        for level, f, gamma, beta, w in (
            (0, f0, gamma0, beta0, w0), (1, f1, gamma1, beta1, w1), (3, f3, gamma3, beta3, w3)
        ):
            gain, bias = load_parameters(gamma, beta, w, level)
            channels = f.rearrange("(c k) n -> k c n", c=P)
            for k in range(f.shape[0] // P):
                block = raws.tile([P, POINTS], F32, name="raw")
                width = (2 if len(raw) in (0, 1, DENSE - 1) else 4) * STAT
                starts = list(range(0, POINTS, width))
                if len(raw) == DENSE - 1:
                    starts.append(POINTS - width // 2)
                for first, end in zip(starts, starts[1:] + [POINTS]):
                    nc.sync.dma_start(block[:, first:end], channels[k, :, first:end])
                if not raw:
                    offsets = held.tile([P, POINTS // 16], U16, name="offsets")
                    nc.sync.dma_start(offsets[:], offs)
                    table_weights = load_weights(w2, 2)
                if k == 0:
                    weights = load_weights(w, level)
                raw.append(block)
                gain_of.append(gain[:, k : k + 1])
                bias_of.append(bias[:, k : k + 1])
                weights_of.append(weights[:, k, :])

        identity = held.tile([P, P], BF16, name="identity")
        make_identity(nc, identity[:])
        eps = held.tile([P, 1], F32, name="eps")
        nc.vector.memset(eps[:], EPS)
        first_use = held.tile([P, 1], F32, name="first_use")
        nc.scalar.activation(first_use[:], eps[:], RSQRT)

        window = held.tile([P, COARSE], BF16, name="window")
        total = [held.tile([P, POINTS], F32, name=f"total{half}") for half in range(2)]

        def scale_and_shift(mean, spread, share, gain, minus_gain, bias, slot):
            columns = scales.tile([P, 4], F32, name=slot)
            minus_mean_gain, rstd, scale, shift = (columns[:, i : i + 1] for i in range(4))
            nc.scalar.activation(rstd, spread, RSQRT, bias=eps[:], scale=share)
            nc.scalar.activation(minus_mean_gain, mean, IDENTITY, scale=minus_gain)
            nc.scalar.activation(shift, rstd, IDENTITY, bias=bias, scale=minus_mean_gain)
            nc.scalar.activation(scale, rstd, IDENTITY, scale=gain)
            return scale, shift

        stats = [held.tile([P, 6 * CHUNKS], F32, name=f"stats{k}") for k in range(DENSE)]

        unused = held.tile([P, COARSE], BF16, name="unused")

        def chunk_statistics(k, c):
            nc.vector.bn_stats(
                stats[k][:, 6 * c : 6 * c + 6], raw[k][:, c * STAT : (c + 1) * STAT]
            )

        def first_chunk_by_scalar(k):
            chunk = raw[k][:, :STAT]
            mean, squares = stats[k][:, 4:5], stats[k][:, 5:6]
            nc.scalar.activation(unused[:, :STAT], chunk, COPY, scale=1.0 / STAT, accum_out=mean)
            nc.scalar.activation(
                unused[:, :STAT], chunk, SQUARE, bias=mean, scale=-1.0, accum_out=squares
            )

        shared = range(SECOND + 1, DENSE)
        for k in shared:
            nc.vector.memset(stats[k][:, 3:4], STAT)

        def normalised(k):
            minus_gain = small.tile([P, 1], F32, name="minus_gain")
            nc.vector.tensor_scalar_mul(minus_gain[:], gain_of[k], -1.0)
            if k == 0:
                chunk_statistics(0, 0)
            for c in range(2 if k in shared else 1, CHUNKS):
                chunk_statistics(k, c)
            if k + 1 < DENSE:
                chunk_statistics(k + 1, 1 if k + 1 in shared else 0)
            mean_var = small.tile([P, 2], F32, name="mean_var")
            nc.vector.bn_aggr(mean_var[:], stats[k][:, 3 if k in shared else 0 :])
            scale, shift = scale_and_shift(
                mean_var[:, 0:1], mean_var[:, 1:2], 1.0, gain_of[k], minus_gain[:], bias_of[k],
                slot="first_columns" if k == 0 else f"columns{k}",
            )
            block = normed.tile([P, POINTS], BF16, name="y")
            by_scalar, by_gpsimd = (FAR, [NEAR]) if FIRST <= k < SECOND else (NEAR, [FAR])
            if k == SECOND:
                by_scalar, by_gpsimd = [], [NEAR, FAR]
            elif k == DENSE - 1:
                by_scalar = [*NEAR[:2], *FAR[:2]]
                by_gpsimd = [NEAR[2:], FAR[2:]]
            for j in by_scalar:
                points = slice(j * PIECE, (j + 1) * PIECE)
                nc.scalar.activation(
                    block[:, points], raw[k][:, points], IDENTITY, bias=shift, scale=scale
                )
            for pieces in by_gpsimd:
                points = slice(pieces[0] * PIECE, (pieces[-1] + 1) * PIECE)
                nc.gpsimd.tensor_scalar(
                    block[:, points], raw[k][:, points], scale, shift, MULT, ADD
                )
            return block

        with tc.psum_pool(name="flips", bufs=1) as flips:
            flipped = flips.tile([P, COARSE], BF16, name="flipped")
            for g in range(COARSE // P):
                nc.tensor.transpose(
                    flipped[:, g * P : (g + 1) * P], table_rows[:, g, :], identity[:]
                )
            mean = small.tile([P, 1], F32, name="mean")
            nc.scalar.activation(
                unused[:], flipped[:], COPY, scale=1.0 / COARSE, accum_out=mean[:]
            )
            spread = small.tile([P, 1], F32, name="spread")
            nc.scalar.activation(
                unused[:], flipped[:], SQUARE, bias=mean[:], scale=-1.0, accum_out=spread[:]
            )
            minus_gain = small.tile([P, 1], F32, name="minus_gain")
            nc.vector.tensor_scalar_mul(minus_gain[:], table_gain[:], -1.0)
            scale, shift = scale_and_shift(
                mean[:], spread[:], 1.0 / COARSE, table_gain[:], minus_gain[:], table_bias[:],
                slot="first_columns",
            )
            nc.scalar.activation(
                window[:].rearrange("d (p g) -> d p g", p=P),
                flipped[:].rearrange("d (g p) -> d p g", p=P),
                IDENTITY, bias=shift, scale=scale,
            )

        with tc.psum_pool(name="sums", bufs=PIECES) as sums:

            def open_banks(pieces):
                return [
                    (sums.tile([P, PIECE], F32, name="bank"), half, j)
                    for j in pieces for half in range(2)
                ]

            def gathered(bank, half, j, start):
                listed = offsets[:, j * (PIECE // 16) : (j + 1) * (PIECE // 16)]
                nc.tensor.matmul(
                    bank[:], table_weights[:, 0, half * P : (half + 1) * P],
                    window[:].indirect(listed), start=start, stop=False,
                )

            def dense(bank, half, j, k, start, stop):
                nc.tensor.matmul(
                    bank[:], weights_of[k][:, half * P : (half + 1) * P],
                    y[k][:, j * PIECE : (j + 1) * PIECE], start=start, stop=stop,
                )

            def park(bank, half, j):
                nc.scalar.copy(total[half][:, j * PIECE : (j + 1) * PIECE], bank[:])

            def finish(bank, half, j):
                points = slice(j * PIECE, (j + 1) * PIECE)
                nc.vector.tensor_tensor(
                    total[half][:, points], bank[:], total[half][:, points], ADD
                )
                nc.sync.dma_start(out[half * P : (half + 1) * P, points], total[half][:, points])

            def finish_by_others(bank, half, j):
                points = slice(j * PIECE, (j + 1) * PIECE)
                late = small.tile([P, PIECE], F32, name="late")
                nc.scalar.copy(late[:], bank[:])
                nc.gpsimd.tensor_tensor(
                    total[half][:, points], late[:], total[half][:, points], ADD
                )
                nc.scalar.dma_start(out[half * P : (half + 1) * P, points], total[half][:, points])


            banks = open_banks(NEAR)
            for bank, half, j in banks:
                gathered(bank, half, j, start=True)
            y = [normalised(k) for k in range(FIRST)]
            for bank, half, j in banks:
                for k in range(FIRST):
                    dense(bank, half, j, k, start=False, stop=(k == FIRST - 1))
                park(bank, half, j)

            for k in range(FIRST, SECOND):
                y.append(normalised(k))
            banks = open_banks(FAR)
            for k in range(FIRST):
                for bank, half, j in banks:
                    dense(bank, half, j, k, start=(k == 0), stop=False)
            for bank, half, j in banks:
                gathered(bank, half, j, start=False)
            for bank, half, j in banks:
                for k in range(FIRST, SECOND):
                    dense(bank, half, j, k, start=False, stop=(k == SECOND - 1))
                park(bank, half, j)
                if (half, j) == (1, FAR[1]):
                    y.append(normalised(SECOND))

            for k in shared:
                first_chunk_by_scalar(k)
                y.append(normalised(k))
            banks = open_banks(NEAR)
            for bank, half, j in banks:
                for k in range(FIRST, DENSE):
                    dense(bank, half, j, k, start=(k == FIRST), stop=(k == DENSE - 1))
                finish(bank, half, j)

            banks = open_banks(FAR)
            for bank, half, j in banks:
                for k in range(SECOND, DENSE):
                    dense(bank, half, j, k, start=(k == SECOND), stop=(k == DENSE - 1))
                if half == 1 and j in FAR[:2]:
                    finish_by_others(bank, half, j)
                else:
                    finish(bank, half, j)
